import numpy as np
import ml_dtypes


def mxq(x, axis, fmt="e4m3"):
    dtype, down = {"e4m3": (ml_dtypes.float8_e4m3fn, 7), "e5m2": (ml_dtypes.float8_e5m2, 14)}[fmt]
    v = np.moveaxis(np.asarray(x, np.float32).astype(ml_dtypes.bfloat16).astype(np.float64), axis, -1)
    blocks = v.reshape(v.shape[:-1] + (-1, 32))
    amax = np.abs(blocks).max(-1, keepdims=True)
    byte = np.maximum(np.where(amax > 0, np.frexp(amax)[1] - 1 + 127, 0) - down, 1)
    scale = np.exp2(byte - 127.0)
    codes = (blocks / scale).astype(np.float32).astype(dtype).astype(np.float64)
    return np.moveaxis((codes * scale).reshape(v.shape), -1, axis)


WIDE = False


def mx_kscale(k):
    if not WIDE:
        return np.ones(k)
    levels = np.array([10, -10, 5, -5, 0])
    a = np.random.permutation(np.resize(levels, k // 512 * 4)).reshape(k // 512, 4)
    idx = np.arange(k)
    return np.exp2(a[idx // 512, idx % 128 // 32])


BF16 = ml_dtypes.bfloat16


def bf(x):
    return np.asarray(x, np.float32).astype(BF16)


def f64(x):
    return np.asarray(x).astype(np.float64)


B, N, D, L = 1, 1024, 512, 512
SEGS = N // L


def setup_inputs():
    t = mx_kscale(D)
    return {"q": bf(np.random.standard_normal((B, N, D)) * 2.0 / np.sqrt(D)),
            "keys_lm": bf(np.random.standard_normal((B, L, D))),
            "vals_lm": bf(np.random.standard_normal((B, L, D)) / np.sqrt(SEGS) * t),
            "v": bf(np.random.standard_normal((B, N, D))),
            "w_proj": bf(np.random.standard_normal((D, D)) * 4.0 / np.sqrt(D) / t[:, None]),
            "b_proj": bf(np.random.standard_normal(D) * 0.1)}


def reference(q, keys_lm, vals_lm, v, w_proj, b_proj):
    s = f64(q) @ f64(keys_lm).transpose(0, 2, 1)
    e = np.exp(s - s.max(-1, keepdims=True))
    o = (mxq(e, 2, "e4m3") @ mxq(f64(vals_lm), 1, "e4m3")) / e.sum(-1, keepdims=True)
    return f64(v) + ((mxq(o, 2, "e4m3") @ mxq(f64(w_proj), 0, "e4m3")) + f64(b_proj))

@@ -1,0 +1,241 @@
+from contextlib import ExitStack
+
+import concourse.mybir as mybir
+from concourse.masks import make_identity
+
+F32 = mybir.dt.float32
+BF16 = mybir.dt.bfloat16
+U32 = mybir.dt.uint32
+U8 = mybir.dt.uint8
+FP8X4 = mybir.dt.float8_e4m3fn_x4
+ALU = mybir.AluOpType
+ACT = mybir.ActivationFunctionType
+AX = mybir.AxisListType
+
+P = 128
+TOKENS = 1024
+D = 512
+L = 512
+NT = TOKENS // P
+FLOPS = 3 * 2 * TOKENS * D * L
+
+LAG_T = 2
+LAG_PV = 3
+LAG_PJ = 4
+
+
+def tile_ammattention_pb_kernel(tc, q, keys_lm, vals_lm, v, w_proj, b_proj, out):
+    nc = tc.nc
+    with ExitStack() as ctx:
+        const = ctx.enter_context(tc.tile_pool(name="const", bufs=1))
+        work = ctx.enter_context(tc.tile_pool(name="work", bufs=3))
+        deep = ctx.enter_context(tc.tile_pool(name="deep", bufs=4))
+        ps_s = ctx.enter_context(tc.psum_pool(name="ps_s", bufs=3))
+        ps_t = ctx.enter_context(tc.psum_pool(name="ps_t", bufs=2))
+        ps_r = ctx.enter_context(tc.psum_pool(name="ps_r", bufs=1))
+        ps_o = ctx.enter_context(tc.psum_pool(name="ps_o", bufs=1))
+        ps_y = ctx.enter_context(tc.psum_pool(name="ps_y", bufs=1))
+        ctx.enter_context(tc.manual_schedule())
+
+        q_v = q.flatten_outer_dims().rearrange("(p a) d -> p a d", a=NT)
+        k_v = keys_lm.flatten_outer_dims().rearrange("(p a) d -> p a d", a=4)
+        val_v = vals_lm.flatten_outer_dims().rearrange("(p j) d -> p j d", j=4)
+        v_v = v.flatten_outer_dims().rearrange("(p a) d -> p a d", a=NT)
+        w_v = w_proj.rearrange("(t p) n -> p t n", p=P)
+        out_v = out.flatten_outer_dims().rearrange("(p a) d -> p a d", a=NT)
+
+        k_raw = const.tile([P, 4 * D], BF16)
+        q_raw = const.tile([P, NT * D], BF16)
+        val_raw = const.tile([P, 4 * D], BF16)
+        w_raw = const.tile([P, 4 * D], BF16)
+        v_raw = const.tile([P, NT * D], BF16)
+        b_row = const.tile([P, D], BF16)
+        k3 = k_raw[:].rearrange("p (a d) -> p a d", a=4)
+        q3 = q_raw[:].rearrange("p (a d) -> p a d", a=NT)
+        v3 = v_raw[:].rearrange("p (a d) -> p a d", a=NT)
+
+        nc.vector.memset(b_row[:], 0.0)
+        nc.sync.dma_start(out=k3[:, 0:2, :], in_=k_v[:, 0:2, :])
+        nc.sync.dma_start(out=k3[:, 2:4, :], in_=k_v[:, 2:4, :])
+        nc.sync.dma_start(out=q3[:, 0:2, :], in_=q_v[:, 0:2, :])
+        nc.sync.dma_start(out=q3[:, 2:8, :], in_=q_v[:, 2:8, :])
+        nc.sync.dma_start(out=b_row[0:1, :], in_=b_proj.unsqueeze(0))
+        nc.sync.dma_start(out=val_raw[:].rearrange("p (j d) -> p j d", j=4), in_=val_v)
+        nc.sync.dma_start(out=w_raw[:].rearrange("p (t n) -> p t n", t=4), in_=w_v)
+        nc.sync.dma_start(out=v3[:, 0:4, :], in_=v_v[:, 0:4, :])
+        nc.sync.dma_start(out=v3[:, 4:8, :], in_=v_v[:, 4:8, :])
+
+        ident_f = const.tile([P, P], F32)
+        make_identity(nc, ident_f[:])
+        ident_b = const.tile([P, P], BF16)
+        make_identity(nc, ident_b[:])
+        ones_b = const.tile([P, P], BF16)
+        nc.vector.memset(ones_b[:], 1.0)
+        warm_in = const.tile([P, 1], F32)
+        warm_out = const.tile([P, 1], F32)
+        nc.vector.memset(warm_in[:], 0.0)
+        nc.scalar.activation(out=warm_out[:], in_=warm_in[:], func=ACT.Exp)
+
+        kT = const.tile([P, 2 * L], F32)
+        k_w = k_raw[:].bitcast(F32)
+        k_ps0 = ps_t.tile([P, L], F32, tag="tp")
+        k_ps1 = ps_t.tile([P, L], F32, tag="tp")
+        k_ps = [k_ps0, k_ps1]
+        for half in range(2):
+            for u in range(2):
+                for a in (2 * half, 2 * half + 1):
+                    nc.tensor.transpose(
+                        k_ps[u][:, a * P:(a + 1) * P],
+                        k_w[:, a * 256 + u * P:a * 256 + (u + 1) * P],
+                        ident_f[:],
+                    )
+        nc.vector.tensor_copy(out=kT[:, 0:L], in_=k_ps0[:])
+        nc.scalar.copy(out=kT[:, L:2 * L], in_=k_ps1[:])
+        kT_b = kT[:].bitcast(BF16).rearrange("p (u c e) -> p u c e", u=2, e=2)
+
+        qT = const.tile([P, NT * 2 * P], F32)
+        q_w = q_raw[:].bitcast(F32)
+        qT_b = qT[:].bitcast(BF16).rearrange("p (a u n e) -> p a u n e", a=NT, u=2, e=2)
+
+        def q_pair(g):
+            if g == 0:
+                q_ps = ps_o.tile([P, 4 * P], F32, tag="o")
+            else:
+                q_ps = ps_t.tile([P, 4 * P], F32, tag="tp")
+            for h in range(2):
+                a = 2 * g + h
+                for u in range(2):
+                    nc.tensor.transpose(
+                        q_ps[:, (2 * h + u) * P:(2 * h + u + 1) * P],
+                        q_w[:, a * 256 + u * P:a * 256 + (u + 1) * P],
+                        ident_f[:],
+                    )
+            if g == 0:
+                nc.vector.tensor_copy(out=qT[:, 0:4 * P], in_=q_ps[:])
+            else:
+                nc.scalar.copy(out=qT[:, g * 4 * P:(g + 1) * 4 * P], in_=q_ps[:])
+
+        q_pair(0)
+
+        val_g = const.tile([P, 4 * D], BF16, align_bytes=64)
+        val_codes = const.tile([P, D], U32, align_bytes=64)
+        val_scales = const.tile([P, D], U8, align_bytes=64)
+        w_g = const.tile([P, 4 * D], BF16, align_bytes=64)
+        w_codes = const.tile([P, D], U32, align_bytes=64)
+        w_scales = const.tile([P, D], U8, align_bytes=64)
+
+        def regroup(grouped, raw):
+            nc.vector.tensor_copy(
+                out=grouped[:].rearrange("p (c i t) -> p c t i", i=4, t=4),
+                in_=raw[:].rearrange("p (t c i) -> p c t i", t=4, i=4),
+            )
+
+        b_all = const.tile([P, D], BF16)
+        vb = const.tile([P, NT * D], F32)
+
+        s_ps = {}
+        negmax = {}
+        rowsum = {}
+        rinv = {}
+        e_bf = {}
+        eT_ps = {}
+        r_ps = {}
+        r_sb = {}
+        e_g = {}
+        e_codes = {}
+        e_scales = {}
+        o_ps = {}
+        o_g = {}
+        o_codes = {}
+        o_scales = {}
+        y_ps = {}
+
+        def live(a):
+            return 0 <= a < NT
+
+        for r in range(NT + LAG_PJ):
+            a0 = r
+            a1 = r - 1
+            at = r - LAG_T
+            av = r - LAG_PV
+            aj = r - LAG_PJ
+            if live(a0):
+                s_ps[a0] = ps_s.tile([P, L], F32, tag="s", name="s_ps")
+                for c in range(4):
+                    nc.tensor.matmul(
+                        s_ps[a0][:], lhsT=qT_b[:, a0, c // 2, :, c % 2], rhs=kT_b[:, c // 2, :, c % 2],
+                        start=(c == 0), stop=(c == 3),
+                    )
+                negmax[a0] = deep.tile([P, 1], F32, tag="negmax", name="negmax")
+                nc.vector.tensor_reduce(out=negmax[a0][:], in_=s_ps[a0][:], axis=AX.X, op=ALU.max,
+                                        negate=True)
+            if r < 3:
+                q_pair(r + 1)
+            if r == 1:
+                b_ps = ps_y.tile([P, D], F32, tag="y")
+                nc.tensor.matmul(b_ps[:], lhsT=ones_b[:], rhs=b_row[:], start=True, stop=True)
+                nc.scalar.copy(out=b_all[:], in_=b_ps[:])
+            if live(at):
+                eT_ps[at] = ps_t.tile([P, 4, P], BF16, tag="tp", name="eT_ps")
+                for t in range(4):
+                    nc.tensor.transpose(eT_ps[at][:, t, :], e_bf[at][:, t * P:(t + 1) * P], ident_b[:])
+                r_ps[at] = ps_r.tile([P, P], F32, tag="r", name="r_ps")
+                nc.tensor.transpose(r_ps[at][:], rinv[at][:].to_broadcast([P, P]), ident_f[:])
+            if r == 2:
+                nc.vector.quantize_mx(out=val_codes[:].bitcast(FP8X4), scales=val_scales[:], in_=val_g[:])
+            if live(av):
+                o_ps[av] = ps_o.tile([P, 4, P], F32, tag="o", name="o_ps")
+                for j in range(4):
+                    nc.tensor.matmul_mx(
+                        out=o_ps[av][:, j, :],
+                        lhsT=val_codes[:, j * P:(j + 1) * P].bitcast(FP8X4),
+                        lhsT_scale=val_scales[:, j * P:(j + 1) * P],
+                        rhs=e_codes[av][:].bitcast(FP8X4), rhs_scale=e_scales[av][:],
+                        start=True, stop=True,
+                    )
+                o_g[av] = work.tile([P, P, 4], BF16, tag="o_g", align_bytes=64, name="o_g")
+                nc.vector.tensor_tensor(
+                    out=o_g[av][:], in0=o_ps[av][:].rearrange("p t n -> p n t"),
+                    in1=r_sb[av][:].unsqueeze(2).to_broadcast([P, P, 4]), op=ALU.mult,
+                )
+            if live(aj):
+                y_ps[aj] = ps_y.tile([P, D], F32, tag="y", name="y_ps")
+                nc.tensor.matmul_mx(
+                    out=y_ps[aj][:], lhsT=o_codes[aj][:].bitcast(FP8X4), lhsT_scale=o_scales[aj][:],
+                    rhs=w_codes[:].bitcast(FP8X4), rhs_scale=w_scales[:], start=True, stop=True,
+                )
+            if live(at):
+                e_g[at] = work.tile([P, P, 4], BF16, tag="e_g", align_bytes=64, name="e_g")
+                nc.scalar.copy(out=e_g[at][:], in_=eT_ps[at][:].rearrange("p t n -> p n t"))
+                r_sb[at] = work.tile([P, P], F32, tag="r_sb", name="r_sb")
+                nc.scalar.copy(out=r_sb[at][:], in_=r_ps[at][:])
+                e_codes[at] = work.tile([P, P], U32, tag="e_codes", align_bytes=64, name="e_codes")
+                e_scales[at] = work.tile([P, P], U8, tag="e_scales", align_bytes=64, name="e_scales")
+                nc.vector.quantize_mx(out=e_codes[at][:].bitcast(FP8X4), scales=e_scales[at][:],
+                                      in_=e_g[at][:].rearrange("p n t -> p (n t)"))
+            if live(av):
+                o_codes[av] = work.tile([P, P], U32, tag="o_codes", align_bytes=64, name="o_codes")
+                o_scales[av] = work.tile([P, P], U8, tag="o_scales", align_bytes=64, name="o_scales")
+                nc.vector.quantize_mx(out=o_codes[av][:].bitcast(FP8X4), scales=o_scales[av][:],
+                                      in_=o_g[av][:].rearrange("p n t -> p (n t)"))
+            if live(a1):
+                rinv[a1] = deep.tile([P, 1], F32, tag="rinv", name="rinv")
+                nc.vector.reciprocal(out=rinv[a1][:], in_=rowsum[a1][:])
+                nc.gpsimd.tensor_tensor(out=vb[:, a1 * D:(a1 + 1) * D], in0=v_raw[:, a1 * D:(a1 + 1) * D],
+                                        in1=b_all[:], op=ALU.add)
+            if r == 1:
+                regroup(w_g, w_raw)
+            if live(aj):
+                y_sb = work.tile([P, D], F32, tag="y_sb")
+                nc.vector.tensor_tensor(out=y_sb[:], in0=y_ps[aj][:], in1=vb[:, aj * D:(aj + 1) * D],
+                                        op=ALU.add)
+                nc.sync.dma_start(out=out_v[:, aj, :], in_=y_sb[:])
+            if r == 0:
+                regroup(val_g, val_raw)
+            if r == 2:
+                nc.vector.quantize_mx(out=w_codes[:].bitcast(FP8X4), scales=w_scales[:], in_=w_g[:])
+            if live(a0):
+                e_bf[a0] = deep.tile([P, L], BF16, tag="e_bf", name="e_bf")
+                rowsum[a0] = deep.tile([P, 1], F32, tag="rowsum", name="rowsum")
+                nc.scalar.activation(out=e_bf[a0][:], in_=s_ps[a0][:], func=ACT.Exp, bias=negmax[a0][:],
+                                     scale=1.0, accum_out=rowsum[a0][:])

@@ -56,9 +56,10 @@ def tile_ammattention_pb_kernel(tc, q, keys_lm, vals_lm, v, w_proj, b_proj, out)
 
         nc.vector.memset(b_row[:], 0.0)
         nc.sync.dma_start(out=k3[:, 0:2, :], in_=k_v[:, 0:2, :])
+        nc.sync.dma_start(out=q3[:, 0:1, :], in_=q_v[:, 0:1, :])
         nc.sync.dma_start(out=k3[:, 2:4, :], in_=k_v[:, 2:4, :])
-        nc.sync.dma_start(out=q3[:, 0:2, :], in_=q_v[:, 0:2, :])
-        nc.sync.dma_start(out=q3[:, 2:8, :], in_=q_v[:, 2:8, :])
+        nc.sync.dma_start(out=q3[:, 1:4, :], in_=q_v[:, 1:4, :])
+        nc.sync.dma_start(out=q3[:, 4:8, :], in_=q_v[:, 4:8, :])
         nc.sync.dma_start(out=b_row[0:1, :], in_=b_proj.unsqueeze(0))
         nc.sync.dma_start(out=val_raw[:].rearrange("p (j d) -> p j d", j=4), in_=val_v)
         nc.sync.dma_start(out=w_raw[:].rearrange("p (t n) -> p t n", t=4), in_=w_v)
@@ -78,44 +79,38 @@ def tile_ammattention_pb_kernel(tc, q, keys_lm, vals_lm, v, w_proj, b_proj, out)
 
         kT = const.tile([P, 2 * L], F32)
         k_w = k_raw[:].bitcast(F32)
-        k_ps0 = ps_t.tile([P, L], F32, tag="tp")
-        k_ps1 = ps_t.tile([P, L], F32, tag="tp")
-        k_ps = [k_ps0, k_ps1]
-        for half in range(2):
-            for u in range(2):
-                for a in (2 * half, 2 * half + 1):
-                    nc.tensor.transpose(
-                        k_ps[u][:, a * P:(a + 1) * P],
-                        k_w[:, a * 256 + u * P:a * 256 + (u + 1) * P],
-                        ident_f[:],
-                    )
-        nc.vector.tensor_copy(out=kT[:, 0:L], in_=k_ps0[:])
-        nc.scalar.copy(out=kT[:, L:2 * L], in_=k_ps1[:])
-        kT_b = kT[:].bitcast(BF16).rearrange("p (u c e) -> p u c e", u=2, e=2)
-
         qT = const.tile([P, NT * 2 * P], F32)
         q_w = q_raw[:].bitcast(F32)
+
+        def q_tile(a, pool, tag):
+            q_ps = pool.tile([P, 2 * P], F32, tag=tag, name="q_ps")
+            for u in range(2):
+                nc.tensor.transpose(q_ps[:, u * P:(u + 1) * P],
+                                    q_w[:, a * 256 + u * P:a * 256 + (u + 1) * P], ident_f[:])
+            return q_ps
+
+        def k_half(half, pools):
+            for u in range(2):
+                pool, tag = pools[u]
+                k_ps = pool.tile([P, 2 * P], F32, tag=tag, name="k_ps")
+                for h in range(2):
+                    a = 2 * half + h
+                    nc.tensor.transpose(k_ps[:, h * P:(h + 1) * P],
+                                        k_w[:, a * 256 + u * P:a * 256 + (u + 1) * P], ident_f[:])
+                dst = kT[:, u * L + 2 * half * P:u * L + (2 * half + 2) * P]
+                if u == 0:
+                    nc.vector.tensor_copy(out=dst, in_=k_ps[:])
+                else:
+                    nc.scalar.copy(out=dst, in_=k_ps[:])
+
+        k_half(0, [(ps_t, "tp"), (ps_t, "tp")])
+        q_ps0 = q_tile(0, ps_r, "r")
+        nc.vector.tensor_copy(out=qT[:, 0:2 * P], in_=q_ps0[:])
+        k_half(1, [(ps_o, "o"), (ps_y, "y")])
+        q_ps1 = q_tile(1, ps_t, "tp")
+        nc.scalar.copy(out=qT[:, 2 * P:4 * P], in_=q_ps1[:])
+        kT_b = kT[:].bitcast(BF16).rearrange("p (u c e) -> p u c e", u=2, e=2)
         qT_b = qT[:].bitcast(BF16).rearrange("p (a u n e) -> p a u n e", a=NT, u=2, e=2)
-
-        def q_pair(g):
-            if g == 0:
-                q_ps = ps_o.tile([P, 4 * P], F32, tag="o")
-            else:
-                q_ps = ps_t.tile([P, 4 * P], F32, tag="tp")
-            for h in range(2):
-                a = 2 * g + h
-                for u in range(2):
-                    nc.tensor.transpose(
-                        q_ps[:, (2 * h + u) * P:(2 * h + u + 1) * P],
-                        q_w[:, a * 256 + u * P:a * 256 + (u + 1) * P],
-                        ident_f[:],
-                    )
-            if g == 0:
-                nc.vector.tensor_copy(out=qT[:, 0:4 * P], in_=q_ps[:])
-            else:
-                nc.scalar.copy(out=qT[:, g * 4 * P:(g + 1) * 4 * P], in_=q_ps[:])
-
-        q_pair(0)
 
         val_g = const.tile([P, 4 * D], BF16, align_bytes=64)
         val_codes = const.tile([P, D], U32, align_bytes=64)
@@ -169,8 +164,9 @@ def tile_ammattention_pb_kernel(tc, q, keys_lm, vals_lm, v, w_proj, b_proj, out)
                 negmax[a0] = deep.tile([P, 1], F32, tag="negmax", name="negmax")
                 nc.vector.tensor_reduce(out=negmax[a0][:], in_=s_ps[a0][:], axis=AX.X, op=ALU.max,
                                         negate=True)
-            if r < 3:
-                q_pair(r + 1)
+            if r + 2 < NT:
+                q_psr = q_tile(r + 2, ps_t, "tp")
+                nc.scalar.copy(out=qT[:, (r + 2) * 2 * P:(r + 3) * 2 * P], in_=q_psr[:])
             if r == 1:
                 b_ps = ps_y.tile([P, D], F32, tag="y")
                 nc.tensor.matmul(b_ps[:], lhsT=ones_b[:], rhs=b_row[:], start=True, stop=True)
@@ -221,8 +217,10 @@ def tile_ammattention_pb_kernel(tc, q, keys_lm, vals_lm, v, w_proj, b_proj, out)
             if live(a1):
                 rinv[a1] = deep.tile([P, 1], F32, tag="rinv", name="rinv")
                 nc.vector.reciprocal(out=rinv[a1][:], in_=rowsum[a1][:])
-                nc.gpsimd.tensor_tensor(out=vb[:, a1 * D:(a1 + 1) * D], in0=v_raw[:, a1 * D:(a1 + 1) * D],
-                                        in1=b_all[:], op=ALU.add)
+                for c in range(4):
+                    lo = a1 * D + c * P
+                    nc.gpsimd.tensor_tensor(out=vb[:, lo:lo + P], in0=v_raw[:, lo:lo + P],
+                                            in1=b_all[:, c * P:(c + 1) * P], op=ALU.add)
             if r == 1:
                 regroup(w_g, w_raw)
             if live(aj):

@@ -19,6 +19,7 @@ L = 512
 NT = TOKENS // P
 FLOPS = 3 * 2 * TOKENS * D * L
 
+N_WARM = 4
 LAG_T = 2
 LAG_PV = 3
 LAG_PJ = 4
@@ -54,6 +55,11 @@ def tile_ammattention_pb_kernel(tc, q, keys_lm, vals_lm, v, w_proj, b_proj, out)
         q3 = q_raw[:].rearrange("p (a d) -> p a d", a=NT)
         v3 = v_raw[:].rearrange("p (a d) -> p a d", a=NT)
 
+        warm_codes = const.tile([P, D], U32, align_bytes=64)
+        warm_scales = const.tile([P, D], U8, align_bytes=64)
+        warm_bf = const.tile([P, 4 * D], BF16, align_bytes=64)
+        nc.vector.memset(warm_bf[:], 0.0)
+        nc.vector.quantize_mx(out=warm_codes[:].bitcast(FP8X4), scales=warm_scales[:], in_=warm_bf[:])
         nc.vector.memset(b_row[:], 0.0)
         nc.sync.dma_start(out=k3[:, 0:2, :], in_=k_v[:, 0:2, :])
         nc.sync.dma_start(out=q3[:, 0:1, :], in_=q_v[:, 0:1, :])
@@ -76,6 +82,13 @@ def tile_ammattention_pb_kernel(tc, q, keys_lm, vals_lm, v, w_proj, b_proj, out)
         warm_out = const.tile([P, 1], F32)
         nc.vector.memset(warm_in[:], 0.0)
         nc.scalar.activation(out=warm_out[:], in_=warm_in[:], func=ACT.Exp)
+
+        warm_ps = ps_s.tile([P, L], F32, tag="s")
+        for i in range(N_WARM):
+            nc.tensor.matmul_mx(
+                out=warm_ps[:], lhsT=warm_codes[:, 0:P].bitcast(FP8X4), lhsT_scale=warm_scales[:, 0:P],
+                rhs=warm_codes[:].bitcast(FP8X4), rhs_scale=warm_scales[:], start=True, stop=True,
+            )
 
         kT = const.tile([P, 2 * L], F32)
         k_w = k_raw[:].bitcast(F32)
@@ -106,6 +119,8 @@ def tile_ammattention_pb_kernel(tc, q, keys_lm, vals_lm, v, w_proj, b_proj, out)
         k_half(0, [(ps_t, "tp"), (ps_t, "tp")])
         q_ps0 = q_tile(0, ps_r, "r")
         nc.vector.tensor_copy(out=qT[:, 0:2 * P], in_=q_ps0[:])
+        for i in range(2):
+            nc.tensor.matmul(warm_ps[:], lhsT=ident_b[:], rhs=q_raw[:, 0:D], start=True, stop=True)
         k_half(1, [(ps_o, "o"), (ps_y, "y")])
         q_ps1 = q_tile(1, ps_t, "tp")
         nc.scalar.copy(out=qT[:, 2 * P:4 * P], in_=q_ps1[:])
@@ -225,9 +240,14 @@ def tile_ammattention_pb_kernel(tc, q, keys_lm, vals_lm, v, w_proj, b_proj, out)
                 regroup(w_g, w_raw)
             if live(aj):
                 y_sb = work.tile([P, D], F32, tag="y_sb")
-                nc.vector.tensor_tensor(out=y_sb[:], in0=y_ps[aj][:], in1=vb[:, aj * D:(aj + 1) * D],
-                                        op=ALU.add)
-                nc.sync.dma_start(out=out_v[:, aj, :], in_=y_sb[:])
+                cuts = 2 if aj == NT - 1 else 1
+                wid = D // cuts
+                for c in range(cuts):
+                    nc.vector.tensor_tensor(out=y_sb[:, c * wid:(c + 1) * wid],
+                                            in0=y_ps[aj][:, c * wid:(c + 1) * wid],
+                                            in1=vb[:, aj * D + c * wid:aj * D + (c + 1) * wid], op=ALU.add)
+                    nc.sync.dma_start(out=out_v[:, aj, c * wid:(c + 1) * wid],
+                                      in_=y_sb[:, c * wid:(c + 1) * wid])
             if r == 0:
                 regroup(val_g, val_raw)
             if r == 2:

@@ -19,7 +19,6 @@ L = 512
 NT = TOKENS // P
 FLOPS = 3 * 2 * TOKENS * D * L
 
-N_WARM = 4
 LAG_T = 2
 LAG_PV = 3
 LAG_PJ = 4
@@ -31,6 +30,7 @@ def tile_ammattention_pb_kernel(tc, q, keys_lm, vals_lm, v, w_proj, b_proj, out)
         const = ctx.enter_context(tc.tile_pool(name="const", bufs=1))
         work = ctx.enter_context(tc.tile_pool(name="work", bufs=3))
         deep = ctx.enter_context(tc.tile_pool(name="deep", bufs=4))
+        pace = ctx.enter_context(tc.tile_pool(name="pace", bufs=2))
         ps_s = ctx.enter_context(tc.psum_pool(name="ps_s", bufs=3))
         ps_t = ctx.enter_context(tc.psum_pool(name="ps_t", bufs=2))
         ps_r = ctx.enter_context(tc.psum_pool(name="ps_r", bufs=1))
@@ -55,11 +55,6 @@ def tile_ammattention_pb_kernel(tc, q, keys_lm, vals_lm, v, w_proj, b_proj, out)
         q3 = q_raw[:].rearrange("p (a d) -> p a d", a=NT)
         v3 = v_raw[:].rearrange("p (a d) -> p a d", a=NT)
 
-        warm_codes = const.tile([P, D], U32, align_bytes=64)
-        warm_scales = const.tile([P, D], U8, align_bytes=64)
-        warm_bf = const.tile([P, 4 * D], BF16, align_bytes=64)
-        nc.vector.memset(warm_bf[:], 0.0)
-        nc.vector.quantize_mx(out=warm_codes[:].bitcast(FP8X4), scales=warm_scales[:], in_=warm_bf[:])
         nc.vector.memset(b_row[:], 0.0)
         nc.sync.dma_start(out=k3[:, 0:2, :], in_=k_v[:, 0:2, :])
         nc.sync.dma_start(out=q3[:, 0:1, :], in_=q_v[:, 0:1, :])
@@ -82,13 +77,6 @@ def tile_ammattention_pb_kernel(tc, q, keys_lm, vals_lm, v, w_proj, b_proj, out)
         warm_out = const.tile([P, 1], F32)
         nc.vector.memset(warm_in[:], 0.0)
         nc.scalar.activation(out=warm_out[:], in_=warm_in[:], func=ACT.Exp)
-
-        warm_ps = ps_s.tile([P, L], F32, tag="s")
-        for i in range(N_WARM):
-            nc.tensor.matmul_mx(
-                out=warm_ps[:], lhsT=warm_codes[:, 0:P].bitcast(FP8X4), lhsT_scale=warm_scales[:, 0:P],
-                rhs=warm_codes[:].bitcast(FP8X4), rhs_scale=warm_scales[:], start=True, stop=True,
-            )
 
         kT = const.tile([P, 2 * L], F32)
         k_w = k_raw[:].bitcast(F32)
@@ -119,8 +107,6 @@ def tile_ammattention_pb_kernel(tc, q, keys_lm, vals_lm, v, w_proj, b_proj, out)
         k_half(0, [(ps_t, "tp"), (ps_t, "tp")])
         q_ps0 = q_tile(0, ps_r, "r")
         nc.vector.tensor_copy(out=qT[:, 0:2 * P], in_=q_ps0[:])
-        for i in range(2):
-            nc.tensor.matmul(warm_ps[:], lhsT=ident_b[:], rhs=q_raw[:, 0:D], start=True, stop=True)
         k_half(1, [(ps_o, "o"), (ps_y, "y")])
         q_ps1 = q_tile(1, ps_t, "tp")
         nc.scalar.copy(out=qT[:, 2 * P:4 * P], in_=q_ps1[:])
@@ -141,7 +127,7 @@ def tile_ammattention_pb_kernel(tc, q, keys_lm, vals_lm, v, w_proj, b_proj, out)
             )
 
         b_all = const.tile([P, D], BF16)
-        vb = const.tile([P, NT * D], F32)
+        vb = {}
 
         s_ps = {}
         negmax = {}
@@ -169,6 +155,9 @@ def tile_ammattention_pb_kernel(tc, q, keys_lm, vals_lm, v, w_proj, b_proj, out)
             at = r - LAG_T
             av = r - LAG_PV
             aj = r - LAG_PJ
+            if live(a1):
+                rinv[a1] = deep.tile([P, 1], F32, tag="rinv", name="rinv")
+                nc.vector.reciprocal(out=rinv[a1][:], in_=rowsum[a1][:])
             if live(a0):
                 s_ps[a0] = ps_s.tile([P, L], F32, tag="s", name="s_ps")
                 for c in range(4):
@@ -229,13 +218,6 @@ def tile_ammattention_pb_kernel(tc, q, keys_lm, vals_lm, v, w_proj, b_proj, out)
                 o_scales[av] = work.tile([P, P], U8, tag="o_scales", align_bytes=64, name="o_scales")
                 nc.vector.quantize_mx(out=o_codes[av][:].bitcast(FP8X4), scales=o_scales[av][:],
                                       in_=o_g[av][:].rearrange("p n t -> p (n t)"))
-            if live(a1):
-                rinv[a1] = deep.tile([P, 1], F32, tag="rinv", name="rinv")
-                nc.vector.reciprocal(out=rinv[a1][:], in_=rowsum[a1][:])
-                for c in range(4):
-                    lo = a1 * D + c * P
-                    nc.gpsimd.tensor_tensor(out=vb[:, lo:lo + P], in0=v_raw[:, lo:lo + P],
-                                            in1=b_all[:, c * P:(c + 1) * P], op=ALU.add)
             if r == 1:
                 regroup(w_g, w_raw)
             if live(aj):
@@ -245,9 +227,13 @@ def tile_ammattention_pb_kernel(tc, q, keys_lm, vals_lm, v, w_proj, b_proj, out)
                 for c in range(cuts):
                     nc.vector.tensor_tensor(out=y_sb[:, c * wid:(c + 1) * wid],
                                             in0=y_ps[aj][:, c * wid:(c + 1) * wid],
-                                            in1=vb[:, aj * D + c * wid:aj * D + (c + 1) * wid], op=ALU.add)
+                                            in1=vb[aj][:, c * wid:(c + 1) * wid], op=ALU.add)
                     nc.sync.dma_start(out=out_v[:, aj, c * wid:(c + 1) * wid],
                                       in_=y_sb[:, c * wid:(c + 1) * wid])
+            if live(at):
+                vb[at] = pace.tile([P, D], F32, tag="vb", name="vb")
+                nc.gpsimd.tensor_tensor(out=vb[at][:], in0=v_raw[:, at * D:(at + 1) * D], in1=b_all[:],
+                                        op=ALU.add)
             if r == 0:
                 regroup(val_g, val_raw)
             if r == 2:

@@ -30,7 +30,6 @@ def tile_ammattention_pb_kernel(tc, q, keys_lm, vals_lm, v, w_proj, b_proj, out)
         const = ctx.enter_context(tc.tile_pool(name="const", bufs=1))
         work = ctx.enter_context(tc.tile_pool(name="work", bufs=3))
         deep = ctx.enter_context(tc.tile_pool(name="deep", bufs=4))
-        pace = ctx.enter_context(tc.tile_pool(name="pace", bufs=2))
         ps_s = ctx.enter_context(tc.psum_pool(name="ps_s", bufs=3))
         ps_t = ctx.enter_context(tc.psum_pool(name="ps_t", bufs=2))
         ps_r = ctx.enter_context(tc.psum_pool(name="ps_r", bufs=1))
@@ -127,7 +126,7 @@ def tile_ammattention_pb_kernel(tc, q, keys_lm, vals_lm, v, w_proj, b_proj, out)
             )
 
         b_all = const.tile([P, D], BF16)
-        vb = {}
+        vb = const.tile([P, NT * D], F32)
 
         s_ps = {}
         negmax = {}
@@ -218,6 +217,11 @@ def tile_ammattention_pb_kernel(tc, q, keys_lm, vals_lm, v, w_proj, b_proj, out)
                 o_scales[av] = work.tile([P, P], U8, tag="o_scales", align_bytes=64, name="o_scales")
                 nc.vector.quantize_mx(out=o_codes[av][:].bitcast(FP8X4), scales=o_scales[av][:],
                                       in_=o_g[av][:].rearrange("p n t -> p (n t)"))
+            if live(a1):
+                for c in range(4):
+                    lo = a1 * D + c * P
+                    nc.gpsimd.tensor_tensor(out=vb[:, lo:lo + P], in0=v_raw[:, lo:lo + P],
+                                            in1=b_all[:, c * P:(c + 1) * P], op=ALU.add)
             if r == 1:
                 regroup(w_g, w_raw)
             if live(aj):
@@ -227,13 +231,9 @@ def tile_ammattention_pb_kernel(tc, q, keys_lm, vals_lm, v, w_proj, b_proj, out)
                 for c in range(cuts):
                     nc.vector.tensor_tensor(out=y_sb[:, c * wid:(c + 1) * wid],
                                             in0=y_ps[aj][:, c * wid:(c + 1) * wid],
-                                            in1=vb[aj][:, c * wid:(c + 1) * wid], op=ALU.add)
+                                            in1=vb[:, aj * D + c * wid:aj * D + (c + 1) * wid], op=ALU.add)
                     nc.sync.dma_start(out=out_v[:, aj, c * wid:(c + 1) * wid],
                                       in_=y_sb[:, c * wid:(c + 1) * wid])
-            if live(at):
-                vb[at] = pace.tile([P, D], F32, tag="vb", name="vb")
-                nc.gpsimd.tensor_tensor(out=vb[at][:], in0=v_raw[:, at * D:(at + 1) * D], in1=b_all[:],
-                                        op=ALU.add)
             if r == 0:
                 regroup(val_g, val_raw)
             if r == 2:

@@ -54,6 +54,8 @@ def tile_ammattention_pb_kernel(tc, q, keys_lm, vals_lm, v, w_proj, b_proj, out)
         q3 = q_raw[:].rearrange("p (a d) -> p a d", a=NT)
         v3 = v_raw[:].rearrange("p (a d) -> p a d", a=NT)
 
+        warm_f = const.tile([P, P], F32)
+        nc.vector.memset(warm_f[:], 0.0)
         nc.vector.memset(b_row[:], 0.0)
         nc.sync.dma_start(out=k3[:, 0:2, :], in_=k_v[:, 0:2, :])
         nc.sync.dma_start(out=q3[:, 0:1, :], in_=q_v[:, 0:1, :])
@@ -76,6 +78,14 @@ def tile_ammattention_pb_kernel(tc, q, keys_lm, vals_lm, v, w_proj, b_proj, out)
         warm_out = const.tile([P, 1], F32)
         nc.vector.memset(warm_in[:], 0.0)
         nc.scalar.activation(out=warm_out[:], in_=warm_in[:], func=ACT.Exp)
+
+        warm_ps = ps_s.tile([P, P], F32, tag="s")
+
+        def warm(n):
+            for i in range(n):
+                nc.tensor.matmul(warm_ps[:], lhsT=warm_f[:], rhs=warm_f[:], start=True, stop=True)
+
+        warm(5)
 
         kT = const.tile([P, 2 * L], F32)
         k_w = k_raw[:].bitcast(F32)
@@ -104,8 +114,10 @@ def tile_ammattention_pb_kernel(tc, q, keys_lm, vals_lm, v, w_proj, b_proj, out)
                     nc.scalar.copy(out=dst, in_=k_ps[:])
 
         k_half(0, [(ps_t, "tp"), (ps_t, "tp")])
+        warm(1)
         q_ps0 = q_tile(0, ps_r, "r")
         nc.vector.tensor_copy(out=qT[:, 0:2 * P], in_=q_ps0[:])
+        warm(2)
         k_half(1, [(ps_o, "o"), (ps_y, "y")])
         q_ps1 = q_tile(1, ps_t, "tp")
         nc.scalar.copy(out=qT[:, 2 * P:4 * P], in_=q_ps1[:])

@@ -30,11 +30,11 @@ def tile_ammattention_pb_kernel(tc, q, keys_lm, vals_lm, v, w_proj, b_proj, out)
         const = ctx.enter_context(tc.tile_pool(name="const", bufs=1))
         work = ctx.enter_context(tc.tile_pool(name="work", bufs=3))
         deep = ctx.enter_context(tc.tile_pool(name="deep", bufs=4))
-        ps_s = ctx.enter_context(tc.psum_pool(name="ps_s", bufs=3))
+        ps_s = ctx.enter_context(tc.psum_pool(name="ps_s", bufs=2))
         ps_t = ctx.enter_context(tc.psum_pool(name="ps_t", bufs=2))
         ps_r = ctx.enter_context(tc.psum_pool(name="ps_r", bufs=1))
         ps_o = ctx.enter_context(tc.psum_pool(name="ps_o", bufs=1))
-        ps_y = ctx.enter_context(tc.psum_pool(name="ps_y", bufs=1))
+        ps_y = ctx.enter_context(tc.psum_pool(name="ps_y", bufs=2))
         ctx.enter_context(tc.manual_schedule())
 
         q_v = q.flatten_outer_dims().rearrange("(p a) d -> p a d", a=NT)

@@ -38,8 +38,8 @@ def tile_ammattention_pb_kernel(tc, q, keys_lm, vals_lm, v, w_proj, b_proj, out)
         ctx.enter_context(tc.manual_schedule())
 
         q_v = q.flatten_outer_dims().rearrange("(p a) d -> p a d", a=NT)
-        k_v = keys_lm.flatten_outer_dims().rearrange("(p a) d -> p a d", a=4)
-        val_v = vals_lm.flatten_outer_dims().rearrange("(p j) d -> p j d", j=4)
+        k_v = keys_lm.flatten_outer_dims().rearrange("(a p) d -> p a d", a=4)
+        val_v = vals_lm.flatten_outer_dims().rearrange("(u p e) d -> p u e d", u=2, e=2)
         v_v = v.flatten_outer_dims().rearrange("(p a) d -> p a d", a=NT)
         w_v = w_proj.rearrange("(t p) n -> p t n", p=P)
         out_v = out.flatten_outer_dims().rearrange("(p a) d -> p a d", a=NT)
@@ -63,15 +63,13 @@ def tile_ammattention_pb_kernel(tc, q, keys_lm, vals_lm, v, w_proj, b_proj, out)
         nc.sync.dma_start(out=q3[:, 1:4, :], in_=q_v[:, 1:4, :])
         nc.sync.dma_start(out=q3[:, 4:8, :], in_=q_v[:, 4:8, :])
         nc.sync.dma_start(out=b_row[0:1, :], in_=b_proj.unsqueeze(0))
-        nc.sync.dma_start(out=val_raw[:].rearrange("p (j d) -> p j d", j=4), in_=val_v)
+        nc.sync.dma_start(out=val_raw[:].rearrange("p (u e d) -> p u e d", u=2, e=2), in_=val_v)
         nc.sync.dma_start(out=w_raw[:].rearrange("p (t n) -> p t n", t=4), in_=w_v)
         nc.sync.dma_start(out=v3[:, 0:4, :], in_=v_v[:, 0:4, :])
         nc.sync.dma_start(out=v3[:, 4:8, :], in_=v_v[:, 4:8, :])
 
         ident_f = const.tile([P, P], F32)
         make_identity(nc, ident_f[:])
-        ident_b = const.tile([P, P], BF16)
-        make_identity(nc, ident_b[:])
         ones_b = const.tile([P, P], BF16)
         nc.vector.memset(ones_b[:], 1.0)
         warm_in = const.tile([P, 1], F32)
@@ -187,9 +185,10 @@ def tile_ammattention_pb_kernel(tc, q, keys_lm, vals_lm, v, w_proj, b_proj, out)
                 nc.tensor.matmul(b_ps[:], lhsT=ones_b[:], rhs=b_row[:], start=True, stop=True)
                 nc.scalar.copy(out=b_all[:], in_=b_ps[:])
             if live(at):
-                eT_ps[at] = ps_t.tile([P, 4, P], BF16, tag="tp", name="eT_ps")
-                for t in range(4):
-                    nc.tensor.transpose(eT_ps[at][:, t, :], e_bf[at][:, t * P:(t + 1) * P], ident_b[:])
+                eT_ps[at] = ps_t.tile([P, 2, P], F32, tag="tp", name="eT_ps")
+                e_w = e_bf[at][:].bitcast(F32)
+                for u in range(2):
+                    nc.tensor.transpose(eT_ps[at][:, u, :], e_w[:, u * P:(u + 1) * P], ident_f[:])
                 r_ps[at] = ps_r.tile([P, P], F32, tag="r", name="r_ps")
                 nc.tensor.transpose(r_ps[at][:], rinv[at][:].to_broadcast([P, P]), ident_f[:])
             if r == 2:
@@ -217,7 +216,8 @@ def tile_ammattention_pb_kernel(tc, q, keys_lm, vals_lm, v, w_proj, b_proj, out)
                 )
             if live(at):
                 e_g[at] = work.tile([P, P, 4], BF16, tag="e_g", align_bytes=64, name="e_g")
-                nc.scalar.copy(out=e_g[at][:], in_=eT_ps[at][:].rearrange("p t n -> p n t"))
+                nc.scalar.copy(out=e_g[at][:].rearrange("p n t -> p (n t)").bitcast(F32).rearrange("p (n u) -> p n u", u=2),
+                               in_=eT_ps[at][:].rearrange("p u n -> p n u"))
                 r_sb[at] = work.tile([P, P], F32, tag="r_sb", name="r_sb")
                 nc.scalar.copy(out=r_sb[at][:], in_=r_ps[at][:])
                 e_codes[at] = work.tile([P, P], U32, tag="e_codes", align_bytes=64, name="e_codes")

@@ -21,7 +21,8 @@ FLOPS = 3 * 2 * TOKENS * D * L
 
 LAG_T = 2
 LAG_PV = 3
-LAG_PJ = 4
+LAG_QO = 4
+LAG_PJ = 5
 
 
 def tile_ammattention_pb_kernel(tc, q, keys_lm, vals_lm, v, w_proj, b_proj, out):
@@ -31,8 +32,7 @@ def tile_ammattention_pb_kernel(tc, q, keys_lm, vals_lm, v, w_proj, b_proj, out)
         work = ctx.enter_context(tc.tile_pool(name="work", bufs=3))
         deep = ctx.enter_context(tc.tile_pool(name="deep", bufs=4))
         ps_s = ctx.enter_context(tc.psum_pool(name="ps_s", bufs=2))
-        ps_t = ctx.enter_context(tc.psum_pool(name="ps_t", bufs=2))
-        ps_r = ctx.enter_context(tc.psum_pool(name="ps_r", bufs=1))
+        ps_t = ctx.enter_context(tc.psum_pool(name="ps_t", bufs=3))
         ps_o = ctx.enter_context(tc.psum_pool(name="ps_o", bufs=1))
         ps_y = ctx.enter_context(tc.psum_pool(name="ps_y", bufs=2))
         ctx.enter_context(tc.manual_schedule())
@@ -113,12 +113,9 @@ def tile_ammattention_pb_kernel(tc, q, keys_lm, vals_lm, v, w_proj, b_proj, out)
 
         k_half(0, [(ps_t, "tp"), (ps_t, "tp")])
         warm(1)
-        q_ps0 = q_tile(0, ps_r, "r")
+        q_ps0 = q_tile(0, ps_t, "tp")
         nc.vector.tensor_copy(out=qT[:, 0:2 * P], in_=q_ps0[:])
-        warm(2)
         k_half(1, [(ps_o, "o"), (ps_y, "y")])
-        q_ps1 = q_tile(1, ps_t, "tp")
-        nc.scalar.copy(out=qT[:, 2 * P:4 * P], in_=q_ps1[:])
         kT_b = kT[:].bitcast(BF16).rearrange("p (u c e) -> p u c e", u=2, e=2)
         qT_b = qT[:].bitcast(BF16).rearrange("p (a u n e) -> p a u n e", a=NT, u=2, e=2)
 
@@ -143,56 +140,66 @@ def tile_ammattention_pb_kernel(tc, q, keys_lm, vals_lm, v, w_proj, b_proj, out)
         rowsum = {}
         rinv = {}
         e_bf = {}
-        eT_ps = {}
-        r_ps = {}
+        t_ps = {}
         r_sb = {}
-        e_g = {}
-        e_codes = {}
-        e_scales = {}
+        grouped = {}
+        codes = {}
+        scales = {}
         o_ps = {}
-        o_g = {}
-        o_codes = {}
-        o_scales = {}
         y_ps = {}
 
         def live(a):
             return 0 <= a < NT
+
+        def grouped_tile(r):
+            if r not in grouped:
+                grouped[r] = work.tile([P, 2 * P, 4], BF16, tag="grouped", align_bytes=64, name="grouped")
+            return grouped[r]
 
         for r in range(NT + LAG_PJ):
             a0 = r
             a1 = r - 1
             at = r - LAG_T
             av = r - LAG_PV
+            aq = r - LAG_QO
             aj = r - LAG_PJ
-            if live(a1):
-                rinv[a1] = deep.tile([P, 1], F32, tag="rinv", name="rinv")
-                nc.vector.reciprocal(out=rinv[a1][:], in_=rowsum[a1][:])
             if live(a0):
                 s_ps[a0] = ps_s.tile([P, L], F32, tag="s", name="s_ps")
-                for c in range(4):
-                    nc.tensor.matmul(
-                        s_ps[a0][:], lhsT=qT_b[:, a0, c // 2, :, c % 2], rhs=kT_b[:, c // 2, :, c % 2],
-                        start=(c == 0), stop=(c == 3),
-                    )
+                halves = 2 if a0 == 0 else 1
+                width = L // halves
+                for h in range(halves):
+                    cols = slice(h * width, (h + 1) * width)
+                    for c in range(4):
+                        nc.tensor.matmul(
+                            s_ps[a0][:, cols], lhsT=qT_b[:, a0, c // 2, :, c % 2], rhs=kT_b[:, c // 2, cols, c % 2],
+                            start=(c == 0), stop=(c == 3),
+                        )
                 negmax[a0] = deep.tile([P, 1], F32, tag="negmax", name="negmax")
                 nc.vector.tensor_reduce(out=negmax[a0][:], in_=s_ps[a0][:], axis=AX.X, op=ALU.max,
                                         negate=True)
-            if r + 2 < NT:
-                q_psr = q_tile(r + 2, ps_t, "tp")
-                nc.scalar.copy(out=qT[:, (r + 2) * 2 * P:(r + 3) * 2 * P], in_=q_psr[:])
+            if live(a1):
+                rinv[a1] = deep.tile([P, 1], F32, tag="rinv", name="rinv")
+                nc.vector.reciprocal(out=rinv[a1][:], in_=rowsum[a1][:])
+            q_ps = {}
+            for a in ((1, 2) if r == 0 else (r + 2,)):
+                if a < NT:
+                    q_ps[a] = q_tile(a, ps_t, "tp")
             if r == 1:
                 b_ps = ps_y.tile([P, D], F32, tag="y")
                 nc.tensor.matmul(b_ps[:], lhsT=ones_b[:], rhs=b_row[:], start=True, stop=True)
-                nc.scalar.copy(out=b_all[:], in_=b_ps[:])
             if live(at):
-                eT_ps[at] = ps_t.tile([P, 2, P], F32, tag="tp", name="eT_ps")
+                t_ps[at] = ps_t.tile([P, 3, P], F32, tag="tp", name="t_ps")
                 e_w = e_bf[at][:].bitcast(F32)
                 for u in range(2):
-                    nc.tensor.transpose(eT_ps[at][:, u, :], e_w[:, u * P:(u + 1) * P], ident_f[:])
-                r_ps[at] = ps_r.tile([P, P], F32, tag="r", name="r_ps")
-                nc.tensor.transpose(r_ps[at][:], rinv[at][:].to_broadcast([P, P]), ident_f[:])
-            if r == 2:
-                nc.vector.quantize_mx(out=val_codes[:].bitcast(FP8X4), scales=val_scales[:], in_=val_g[:])
+                    nc.tensor.transpose(t_ps[at][:, u, :], e_w[:, u * P:(u + 1) * P], ident_f[:])
+                nc.tensor.transpose(t_ps[at][:, 2, :], rinv[at][:].to_broadcast([P, P]), ident_f[:])
+            if live(aj):
+                y_ps[aj] = ps_y.tile([P, D], F32, tag="y", name="y_ps")
+                nc.tensor.matmul_mx(
+                    out=y_ps[aj][:], lhsT=codes[aj + LAG_QO][:, P:2 * P].bitcast(FP8X4),
+                    lhsT_scale=scales[aj + LAG_QO][:, P:2 * P],
+                    rhs=w_codes[:].bitcast(FP8X4), rhs_scale=w_scales[:], start=True, stop=True,
+                )
             if live(av):
                 o_ps[av] = ps_o.tile([P, 4, P], F32, tag="o", name="o_ps")
                 for j in range(4):
@@ -200,42 +207,38 @@ def tile_ammattention_pb_kernel(tc, q, keys_lm, vals_lm, v, w_proj, b_proj, out)
                         out=o_ps[av][:, j, :],
                         lhsT=val_codes[:, j * P:(j + 1) * P].bitcast(FP8X4),
                         lhsT_scale=val_scales[:, j * P:(j + 1) * P],
-                        rhs=e_codes[av][:].bitcast(FP8X4), rhs_scale=e_scales[av][:],
+                        rhs=codes[av + LAG_T][:, 0:P].bitcast(FP8X4), rhs_scale=scales[av + LAG_T][:, 0:P],
                         start=True, stop=True,
                     )
-                o_g[av] = work.tile([P, P, 4], BF16, tag="o_g", align_bytes=64, name="o_g")
+            if live(at):
+                g = grouped_tile(r)
+                nc.scalar.copy(out=g[:, 0:P, :].rearrange("p n t -> p (n t)").bitcast(F32).rearrange("p (n u) -> p n u", u=2),
+                               in_=t_ps[at][:, 0:2, :].rearrange("p u n -> p n u"))
+                r_sb[at] = work.tile([P, P], F32, tag="r_sb", name="r_sb")
+                nc.scalar.copy(out=r_sb[at][:], in_=t_ps[at][:, 2, :])
+            for a in q_ps:
+                nc.scalar.copy(out=qT[:, a * 2 * P:(a + 1) * 2 * P], in_=q_ps[a][:])
+            if r == 1:
+                nc.scalar.copy(out=b_all[:], in_=b_ps[:])
+                nc.vector.quantize_mx(out=val_codes[:].bitcast(FP8X4), scales=val_scales[:], in_=val_g[:])
+            if live(at) or live(aq):
+                lo = 0 if live(at) else P
+                hi = 2 * P if live(aq) else P
+                codes[r] = work.tile([P, 2 * P], U32, tag="codes", align_bytes=64, name="codes")
+                scales[r] = work.tile([P, 2 * P], U8, tag="scales", align_bytes=64, name="scales")
+                nc.vector.quantize_mx(out=codes[r][:, lo:hi].bitcast(FP8X4), scales=scales[r][:, lo:hi],
+                                      in_=grouped[r][:, lo:hi, :].rearrange("p n t -> p (n t)"))
+            if live(av):
+                g = grouped_tile(r + 1)
                 nc.vector.tensor_tensor(
-                    out=o_g[av][:], in0=o_ps[av][:].rearrange("p t n -> p n t"),
+                    out=g[:, P:2 * P, :], in0=o_ps[av][:].rearrange("p t n -> p n t"),
                     in1=r_sb[av][:].unsqueeze(2).to_broadcast([P, P, 4]), op=ALU.mult,
                 )
-            if live(aj):
-                y_ps[aj] = ps_y.tile([P, D], F32, tag="y", name="y_ps")
-                nc.tensor.matmul_mx(
-                    out=y_ps[aj][:], lhsT=o_codes[aj][:].bitcast(FP8X4), lhsT_scale=o_scales[aj][:],
-                    rhs=w_codes[:].bitcast(FP8X4), rhs_scale=w_scales[:], start=True, stop=True,
-                )
-            if live(at):
-                e_g[at] = work.tile([P, P, 4], BF16, tag="e_g", align_bytes=64, name="e_g")
-                nc.scalar.copy(out=e_g[at][:].rearrange("p n t -> p (n t)").bitcast(F32).rearrange("p (n u) -> p n u", u=2),
-                               in_=eT_ps[at][:].rearrange("p u n -> p n u"))
-                r_sb[at] = work.tile([P, P], F32, tag="r_sb", name="r_sb")
-                nc.scalar.copy(out=r_sb[at][:], in_=r_ps[at][:])
-                e_codes[at] = work.tile([P, P], U32, tag="e_codes", align_bytes=64, name="e_codes")
-                e_scales[at] = work.tile([P, P], U8, tag="e_scales", align_bytes=64, name="e_scales")
-                nc.vector.quantize_mx(out=e_codes[at][:].bitcast(FP8X4), scales=e_scales[at][:],
-                                      in_=e_g[at][:].rearrange("p n t -> p (n t)"))
-            if live(av):
-                o_codes[av] = work.tile([P, P], U32, tag="o_codes", align_bytes=64, name="o_codes")
-                o_scales[av] = work.tile([P, P], U8, tag="o_scales", align_bytes=64, name="o_scales")
-                nc.vector.quantize_mx(out=o_codes[av][:].bitcast(FP8X4), scales=o_scales[av][:],
-                                      in_=o_g[av][:].rearrange("p n t -> p (n t)"))
             if live(a1):
                 for c in range(4):
                     lo = a1 * D + c * P
                     nc.gpsimd.tensor_tensor(out=vb[:, lo:lo + P], in0=v_raw[:, lo:lo + P],
                                             in1=b_all[:, c * P:(c + 1) * P], op=ALU.add)
-            if r == 1:
-                regroup(w_g, w_raw)
             if live(aj):
                 y_sb = work.tile([P, D], F32, tag="y_sb")
                 cuts = 2 if aj == NT - 1 else 1
@@ -249,6 +252,8 @@ def tile_ammattention_pb_kernel(tc, q, keys_lm, vals_lm, v, w_proj, b_proj, out)
             if r == 0:
                 regroup(val_g, val_raw)
             if r == 2:
+                regroup(w_g, w_raw)
+            if r == 3:
                 nc.vector.quantize_mx(out=w_codes[:].bitcast(FP8X4), scales=w_scales[:], in_=w_g[:])
             if live(a0):
                 e_bf[a0] = deep.tile([P, L], BF16, tag="e_bf", name="e_bf")

@@ -23,6 +23,7 @@ LAG_T = 2
 LAG_PV = 3
 LAG_QO = 4
 LAG_PJ = 5
+W_CUT = D - 3 * 64
 
 
 def tile_ammattention_pb_kernel(tc, q, keys_lm, vals_lm, v, w_proj, b_proj, out):
@@ -61,9 +62,9 @@ def tile_ammattention_pb_kernel(tc, q, keys_lm, vals_lm, v, w_proj, b_proj, out)
         nc.sync.dma_start(out=q3[:, 0:1, :], in_=q_v[:, 0:1, :])
         nc.sync.dma_start(out=k3[:, 2:4, :], in_=k_v[:, 2:4, :])
         nc.sync.dma_start(out=q3[:, 1:4, :], in_=q_v[:, 1:4, :])
-        nc.sync.dma_start(out=q3[:, 4:8, :], in_=q_v[:, 4:8, :])
-        nc.sync.dma_start(out=b_row[0:1, :], in_=b_proj.unsqueeze(0))
         nc.sync.dma_start(out=val_raw[:].rearrange("p (u e d) -> p u e d", u=2, e=2), in_=val_v)
+        nc.sync.dma_start(out=b_row[0:1, :], in_=b_proj.unsqueeze(0))
+        nc.sync.dma_start(out=q3[:, 4:8, :], in_=q_v[:, 4:8, :])
         nc.sync.dma_start(out=w_raw[:].rearrange("p (t n) -> p t n", t=4), in_=w_v)
         nc.sync.dma_start(out=v3[:, 0:4, :], in_=v_v[:, 0:4, :])
         nc.sync.dma_start(out=v3[:, 4:8, :], in_=v_v[:, 4:8, :])
@@ -112,10 +113,10 @@ def tile_ammattention_pb_kernel(tc, q, keys_lm, vals_lm, v, w_proj, b_proj, out)
                     nc.scalar.copy(out=dst, in_=k_ps[:])
 
         k_half(0, [(ps_t, "tp"), (ps_t, "tp")])
-        warm(1)
         q_ps0 = q_tile(0, ps_t, "tp")
         nc.vector.tensor_copy(out=qT[:, 0:2 * P], in_=q_ps0[:])
         k_half(1, [(ps_o, "o"), (ps_y, "y")])
+        warm(1)
         kT_b = kT[:].bitcast(BF16).rearrange("p (u c e) -> p u c e", u=2, e=2)
         qT_b = qT[:].bitcast(BF16).rearrange("p (a u n e) -> p a u n e", a=NT, u=2, e=2)
 
@@ -126,10 +127,10 @@ def tile_ammattention_pb_kernel(tc, q, keys_lm, vals_lm, v, w_proj, b_proj, out)
         w_codes = const.tile([P, D], U32, align_bytes=64)
         w_scales = const.tile([P, D], U8, align_bytes=64)
 
-        def regroup(grouped, raw):
-            nc.vector.tensor_copy(
-                out=grouped[:].rearrange("p (c i t) -> p c t i", i=4, t=4),
-                in_=raw[:].rearrange("p (t c i) -> p c t i", t=4, i=4),
+        def regroup(copy, grouped, raw, lo, hi):
+            copy(
+                out=grouped[:, 4 * lo:4 * hi].rearrange("p (c i t) -> p c t i", i=4, t=4),
+                in_=raw[:].rearrange("p (t n) -> p t n", t=4)[:, :, lo:hi].rearrange("p t (c i) -> p c t i", i=4),
             )
 
         b_all = const.tile([P, D], BF16)
@@ -184,7 +185,7 @@ def tile_ammattention_pb_kernel(tc, q, keys_lm, vals_lm, v, w_proj, b_proj, out)
             for a in ((1, 2) if r == 0 else (r + 2,)):
                 if a < NT:
                     q_ps[a] = q_tile(a, ps_t, "tp")
-            if r == 1:
+            if r == 0:
                 b_ps = ps_y.tile([P, D], F32, tag="y")
                 nc.tensor.matmul(b_ps[:], lhsT=ones_b[:], rhs=b_row[:], start=True, stop=True)
             if live(at):
@@ -218,9 +219,12 @@ def tile_ammattention_pb_kernel(tc, q, keys_lm, vals_lm, v, w_proj, b_proj, out)
                 nc.scalar.copy(out=r_sb[at][:], in_=t_ps[at][:, 2, :])
             for a in q_ps:
                 nc.scalar.copy(out=qT[:, a * 2 * P:(a + 1) * 2 * P], in_=q_ps[a][:])
-            if r == 1:
+            if r == 0:
                 nc.scalar.copy(out=b_all[:], in_=b_ps[:])
+            if r == 1:
                 nc.vector.quantize_mx(out=val_codes[:].bitcast(FP8X4), scales=val_scales[:], in_=val_g[:])
+            if r == 4:
+                nc.vector.quantize_mx(out=w_codes[:].bitcast(FP8X4), scales=w_scales[:], in_=w_g[:])
             if live(at) or live(aq):
                 lo = 0 if live(at) else P
                 hi = 2 * P if live(aq) else P
@@ -250,13 +254,14 @@ def tile_ammattention_pb_kernel(tc, q, keys_lm, vals_lm, v, w_proj, b_proj, out)
                     nc.sync.dma_start(out=out_v[:, aj, c * wid:(c + 1) * wid],
                                       in_=y_sb[:, c * wid:(c + 1) * wid])
             if r == 0:
-                regroup(val_g, val_raw)
+                regroup(nc.vector.tensor_copy, val_g, val_raw, 0, D)
             if r == 2:
-                regroup(w_g, w_raw)
-            if r == 3:
-                nc.vector.quantize_mx(out=w_codes[:].bitcast(FP8X4), scales=w_scales[:], in_=w_g[:])
+                regroup(nc.vector.tensor_copy, w_g, w_raw, 0, W_CUT)
             if live(a0):
                 e_bf[a0] = deep.tile([P, L], BF16, tag="e_bf", name="e_bf")
                 rowsum[a0] = deep.tile([P, 1], F32, tag="rowsum", name="rowsum")
                 nc.scalar.activation(out=e_bf[a0][:], in_=s_ps[a0][:], func=ACT.Exp, bias=negmax[a0][:],
                                      scale=1.0, accum_out=rowsum[a0][:])
+            if 1 <= r <= 3:
+                lo = W_CUT + (r - 1) * 64
+                regroup(nc.scalar.copy, w_g, w_raw, lo, lo + 64)

from contextlib import ExitStack

import concourse.mybir as mybir
from concourse.masks import make_identity

F32 = mybir.dt.float32
BF16 = mybir.dt.bfloat16
U32 = mybir.dt.uint32
U8 = mybir.dt.uint8
FP8X4 = mybir.dt.float8_e4m3fn_x4
ALU = mybir.AluOpType
ACT = mybir.ActivationFunctionType
AX = mybir.AxisListType

P = 128
TOKENS = 1024
D = 512
L = 512
NT = TOKENS // P
FLOPS = 3 * 2 * TOKENS * D * L

LAG_T = 2
LAG_PV = 3
LAG_QO = 4
LAG_PJ = 5
W_CUT = D - 3 * 64


def tile_ammattention_pb_kernel(tc, q, keys_lm, vals_lm, v, w_proj, b_proj, out):
    nc = tc.nc
    with ExitStack() as ctx:
        const = ctx.enter_context(tc.tile_pool(name="const", bufs=1))
        work = ctx.enter_context(tc.tile_pool(name="work", bufs=3))
        deep = ctx.enter_context(tc.tile_pool(name="deep", bufs=4))
        ps_s = ctx.enter_context(tc.psum_pool(name="ps_s", bufs=2))
        ps_t = ctx.enter_context(tc.psum_pool(name="ps_t", bufs=3))
        ps_o = ctx.enter_context(tc.psum_pool(name="ps_o", bufs=1))
        ps_y = ctx.enter_context(tc.psum_pool(name="ps_y", bufs=2))
        ctx.enter_context(tc.manual_schedule())

        q_v = q.flatten_outer_dims().rearrange("(p a) d -> p a d", a=NT)
        k_v = keys_lm.flatten_outer_dims().rearrange("(a p) d -> p a d", a=4)
        val_v = vals_lm.flatten_outer_dims().rearrange("(u p e) d -> p u e d", u=2, e=2)
        v_v = v.flatten_outer_dims().rearrange("(p a) d -> p a d", a=NT)
        w_v = w_proj.rearrange("(t p) n -> p t n", p=P)
        out_v = out.flatten_outer_dims().rearrange("(p a) d -> p a d", a=NT)

        k_raw = const.tile([P, 4 * D], BF16)
        q_raw = const.tile([P, NT * D], BF16)
        val_raw = const.tile([P, 4 * D], BF16)
        w_raw = const.tile([P, 4 * D], BF16)
        v_raw = const.tile([P, NT * D], BF16)
        b_row = const.tile([P, D], BF16)
        k3 = k_raw[:].rearrange("p (a d) -> p a d", a=4)
        q3 = q_raw[:].rearrange("p (a d) -> p a d", a=NT)
        v3 = v_raw[:].rearrange("p (a d) -> p a d", a=NT)

        warm_f = const.tile([P, P], F32)
        nc.vector.memset(warm_f[:], 0.0)
        nc.vector.memset(b_row[:], 0.0)
        nc.sync.dma_start(out=k3[:, 0:2, :], in_=k_v[:, 0:2, :])
        nc.sync.dma_start(out=q3[:, 0:1, :], in_=q_v[:, 0:1, :])
        nc.sync.dma_start(out=k3[:, 2:4, :], in_=k_v[:, 2:4, :])
        nc.sync.dma_start(out=q3[:, 1:4, :], in_=q_v[:, 1:4, :])
        nc.sync.dma_start(out=val_raw[:].rearrange("p (u e d) -> p u e d", u=2, e=2), in_=val_v)
        nc.sync.dma_start(out=b_row[0:1, :], in_=b_proj.unsqueeze(0))
        nc.sync.dma_start(out=q3[:, 4:8, :], in_=q_v[:, 4:8, :])
        nc.sync.dma_start(out=w_raw[:].rearrange("p (t n) -> p t n", t=4), in_=w_v)
        nc.sync.dma_start(out=v3[:, 0:4, :], in_=v_v[:, 0:4, :])
        nc.sync.dma_start(out=v3[:, 4:8, :], in_=v_v[:, 4:8, :])

        ident_f = const.tile([P, P], F32)
        make_identity(nc, ident_f[:])
        ones_b = const.tile([P, P], BF16)
        nc.vector.memset(ones_b[:], 1.0)
        warm_in = const.tile([P, 1], F32)
        warm_out = const.tile([P, 1], F32)
        nc.vector.memset(warm_in[:], 0.0)
        nc.scalar.activation(out=warm_out[:], in_=warm_in[:], func=ACT.Exp)

        warm_ps = ps_s.tile([P, P], F32, tag="s")

        def warm(n):
            for i in range(n):
                nc.tensor.matmul(warm_ps[:], lhsT=warm_f[:], rhs=warm_f[:], start=True, stop=True)

        warm(5)

        kT = const.tile([P, 2 * L], F32)
        k_w = k_raw[:].bitcast(F32)
        qT = const.tile([P, NT * 2 * P], F32)
        q_w = q_raw[:].bitcast(F32)

        def q_tile(a, pool, tag):
            q_ps = pool.tile([P, 2 * P], F32, tag=tag, name="q_ps")
            for u in range(2):
                nc.tensor.transpose(q_ps[:, u * P:(u + 1) * P],
                                    q_w[:, a * 256 + u * P:a * 256 + (u + 1) * P], ident_f[:])
            return q_ps

        def k_half(half, pools):
            for u in range(2):
                pool, tag = pools[u]
                k_ps = pool.tile([P, 2 * P], F32, tag=tag, name="k_ps")
                for h in range(2):
                    a = 2 * half + h
                    nc.tensor.transpose(k_ps[:, h * P:(h + 1) * P],
                                        k_w[:, a * 256 + u * P:a * 256 + (u + 1) * P], ident_f[:])
                dst = kT[:, u * L + 2 * half * P:u * L + (2 * half + 2) * P]
                if u == 0:
                    nc.vector.tensor_copy(out=dst, in_=k_ps[:])
                else:
                    nc.scalar.copy(out=dst, in_=k_ps[:])

        k_half(0, [(ps_t, "tp"), (ps_t, "tp")])
        q_ps0 = q_tile(0, ps_t, "tp")
        nc.vector.tensor_copy(out=qT[:, 0:2 * P], in_=q_ps0[:])
        k_half(1, [(ps_o, "o"), (ps_y, "y")])
        warm(1)
        kT_b = kT[:].bitcast(BF16).rearrange("p (u c e) -> p u c e", u=2, e=2)
        qT_b = qT[:].bitcast(BF16).rearrange("p (a u n e) -> p a u n e", a=NT, u=2, e=2)

        val_g = const.tile([P, 4 * D], BF16, align_bytes=64)
        val_codes = const.tile([P, D], U32, align_bytes=64)
        val_scales = const.tile([P, D], U8, align_bytes=64)
        w_g = const.tile([P, 4 * D], BF16, align_bytes=64)
        w_codes = const.tile([P, D], U32, align_bytes=64)
        w_scales = const.tile([P, D], U8, align_bytes=64)

        def regroup(copy, grouped, raw, lo, hi):
            copy(
                out=grouped[:, 4 * lo:4 * hi].rearrange("p (c i t) -> p c t i", i=4, t=4),
                in_=raw[:].rearrange("p (t n) -> p t n", t=4)[:, :, lo:hi].rearrange("p t (c i) -> p c t i", i=4),
            )

        b_all = const.tile([P, D], BF16)
        vb = const.tile([P, NT * D], F32)

        s_ps = {}
        negmax = {}
        rowsum = {}
        rinv = {}
        e_bf = {}
        t_ps = {}
        r_sb = {}
        grouped = {}
        codes = {}
        scales = {}
        o_ps = {}
        y_ps = {}

        def live(a):
            return 0 <= a < NT

        def grouped_tile(r):
            if r not in grouped:
                grouped[r] = work.tile([P, 2 * P, 4], BF16, tag="grouped", align_bytes=64, name="grouped")
            return grouped[r]

        for r in range(NT + LAG_PJ):
            a0 = r
            a1 = r - 1
            at = r - LAG_T
            av = r - LAG_PV
            aq = r - LAG_QO
            aj = r - LAG_PJ
            if live(a0):
                s_ps[a0] = ps_s.tile([P, L], F32, tag="s", name="s_ps")
                halves = 2 if a0 == 0 else 1
                width = L // halves
                for h in range(halves):
                    cols = slice(h * width, (h + 1) * width)
                    for c in range(4):
                        nc.tensor.matmul(
                            s_ps[a0][:, cols], lhsT=qT_b[:, a0, c // 2, :, c % 2], rhs=kT_b[:, c // 2, cols, c % 2],
                            start=(c == 0), stop=(c == 3),
                        )
                negmax[a0] = deep.tile([P, 1], F32, tag="negmax", name="negmax")
                nc.vector.tensor_reduce(out=negmax[a0][:], in_=s_ps[a0][:], axis=AX.X, op=ALU.max,
                                        negate=True)
            if live(a1):
                rinv[a1] = deep.tile([P, 1], F32, tag="rinv", name="rinv")
                nc.vector.reciprocal(out=rinv[a1][:], in_=rowsum[a1][:])
            q_ps = {}
            for a in ((1, 2) if r == 0 else (r + 2,)):
                if a < NT:
                    q_ps[a] = q_tile(a, ps_t, "tp")
            if r == 0:
                b_ps = ps_y.tile([P, D], F32, tag="y")
                nc.tensor.matmul(b_ps[:], lhsT=ones_b[:], rhs=b_row[:], start=True, stop=True)
            if live(at):
                t_ps[at] = ps_t.tile([P, 3, P], F32, tag="tp", name="t_ps")
                e_w = e_bf[at][:].bitcast(F32)
                for u in range(2):
                    nc.tensor.transpose(t_ps[at][:, u, :], e_w[:, u * P:(u + 1) * P], ident_f[:])
                nc.tensor.transpose(t_ps[at][:, 2, :], rinv[at][:].to_broadcast([P, P]), ident_f[:])
            if live(aj):
                y_ps[aj] = ps_y.tile([P, D], F32, tag="y", name="y_ps")
                nc.tensor.matmul_mx(
                    out=y_ps[aj][:], lhsT=codes[aj + LAG_QO][:, P:2 * P].bitcast(FP8X4),
                    lhsT_scale=scales[aj + LAG_QO][:, P:2 * P],
                    rhs=w_codes[:].bitcast(FP8X4), rhs_scale=w_scales[:], start=True, stop=True,
                )
            if live(av):
                o_ps[av] = ps_o.tile([P, 4, P], F32, tag="o", name="o_ps")
                for j in range(4):
                    nc.tensor.matmul_mx(
                        out=o_ps[av][:, j, :],
                        lhsT=val_codes[:, j * P:(j + 1) * P].bitcast(FP8X4),
                        lhsT_scale=val_scales[:, j * P:(j + 1) * P],
                        rhs=codes[av + LAG_T][:, 0:P].bitcast(FP8X4), rhs_scale=scales[av + LAG_T][:, 0:P],
                        start=True, stop=True,
                    )
            if live(at):
                g = grouped_tile(r)
                nc.scalar.copy(out=g[:, 0:P, :].rearrange("p n t -> p (n t)").bitcast(F32).rearrange("p (n u) -> p n u", u=2),
                               in_=t_ps[at][:, 0:2, :].rearrange("p u n -> p n u"))
                r_sb[at] = work.tile([P, P], F32, tag="r_sb", name="r_sb")
                nc.scalar.copy(out=r_sb[at][:], in_=t_ps[at][:, 2, :])
            for a in q_ps:
                nc.scalar.copy(out=qT[:, a * 2 * P:(a + 1) * 2 * P], in_=q_ps[a][:])
            if r == 0:
                nc.scalar.copy(out=b_all[:], in_=b_ps[:])
            if r == 1:
                nc.vector.quantize_mx(out=val_codes[:].bitcast(FP8X4), scales=val_scales[:], in_=val_g[:])
            if r == 4:
                nc.vector.quantize_mx(out=w_codes[:].bitcast(FP8X4), scales=w_scales[:], in_=w_g[:])
            if live(at) or live(aq):
                lo = 0 if live(at) else P
                hi = 2 * P if live(aq) else P
                codes[r] = work.tile([P, 2 * P], U32, tag="codes", align_bytes=64, name="codes")
                scales[r] = work.tile([P, 2 * P], U8, tag="scales", align_bytes=64, name="scales")
                nc.vector.quantize_mx(out=codes[r][:, lo:hi].bitcast(FP8X4), scales=scales[r][:, lo:hi],
                                      in_=grouped[r][:, lo:hi, :].rearrange("p n t -> p (n t)"))
            if live(av):
                g = grouped_tile(r + 1)
                nc.vector.tensor_tensor(
                    out=g[:, P:2 * P, :], in0=o_ps[av][:].rearrange("p t n -> p n t"),
                    in1=r_sb[av][:].unsqueeze(2).to_broadcast([P, P, 4]), op=ALU.mult,
                )
            if live(a1):
                for c in range(4):
                    lo = a1 * D + c * P
                    nc.gpsimd.tensor_tensor(out=vb[:, lo:lo + P], in0=v_raw[:, lo:lo + P],
                                            in1=b_all[:, c * P:(c + 1) * P], op=ALU.add)
            if live(aj):
                y_sb = work.tile([P, D], F32, tag="y_sb")
                cuts = 2 if aj == NT - 1 else 1
                wid = D // cuts
                for c in range(cuts):
                    nc.vector.tensor_tensor(out=y_sb[:, c * wid:(c + 1) * wid],
                                            in0=y_ps[aj][:, c * wid:(c + 1) * wid],
                                            in1=vb[:, aj * D + c * wid:aj * D + (c + 1) * wid], op=ALU.add)
                    nc.sync.dma_start(out=out_v[:, aj, c * wid:(c + 1) * wid],
                                      in_=y_sb[:, c * wid:(c + 1) * wid])
            if r == 0:
                regroup(nc.vector.tensor_copy, val_g, val_raw, 0, D)
            if r == 2:
                regroup(nc.vector.tensor_copy, w_g, w_raw, 0, W_CUT)
            if live(a0):
                e_bf[a0] = deep.tile([P, L], BF16, tag="e_bf", name="e_bf")
                rowsum[a0] = deep.tile([P, 1], F32, tag="rowsum", name="rowsum")
                nc.scalar.activation(out=e_bf[a0][:], in_=s_ps[a0][:], func=ACT.Exp, bias=negmax[a0][:],
                                     scale=1.0, accum_out=rowsum[a0][:])
            if 1 <= r <= 3:
                lo = W_CUT + (r - 1) * 64
                regroup(nc.scalar.copy, w_g, w_raw, lo, lo + 64)
